import numpy as np
import ml_dtypes


def mxq(x, axis, fmt="e4m3"):
    dtype, down = {"e4m3": (ml_dtypes.float8_e4m3fn, 7), "e5m2": (ml_dtypes.float8_e5m2, 14)}[fmt]
    v = np.moveaxis(np.asarray(x, np.float32).astype(ml_dtypes.bfloat16).astype(np.float64), axis, -1)
    blocks = v.reshape(v.shape[:-1] + (-1, 32))
    amax = np.abs(blocks).max(-1, keepdims=True)
    byte = np.maximum(np.where(amax > 0, np.frexp(amax)[1] - 1 + 127, 0) - down, 1)
    scale = np.exp2(byte - 127.0)
    codes = (blocks / scale).astype(np.float32).astype(dtype).astype(np.float64)
    return np.moveaxis((codes * scale).reshape(v.shape), -1, axis)


WIDE = False


def mx_kscale(k):
    if not WIDE:
        return np.ones(k)
    levels = np.array([10, -10, 5, -5, 0])
    a = np.random.permutation(np.resize(levels, k // 512 * 4)).reshape(k // 512, 4)
    idx = np.arange(k)
    return np.exp2(a[idx // 512, idx % 128 // 32])


BF16 = ml_dtypes.bfloat16


def bf(x):
    return np.asarray(x, np.float32).astype(BF16)


def f64(x):
    return np.asarray(x).astype(np.float64)


E2M1 = np.array([0.0, 0.5, 1.0, 1.5, 2.0, 3.0, 4.0, 6.0, -0.0, -0.5, -1.0, -1.5, -2.0, -3.0, -4.0, -6.0])


def pack_weight(w, fmt):
    k, n = w.shape
    w = f64(bf(w)).reshape(k // 32, 32, n)
    amax = np.abs(w).max(1)
    if fmt == "e4m3":
        byte = np.frexp(amax)[1] - 1 + 127 - 7
    else:
        mant, ex = np.frexp(amax / 6.0)
        byte = np.where(mant > 0.5, ex, ex - 1) + 127
    byte = np.clip(np.where(amax > 0, byte, 1), 1, 254)
    scaled = (w * np.exp2(127.0 - byte)[:, None, :]).reshape(k, n).astype(np.float32)
    by_word = np.ascontiguousarray(scaled.reshape(k // 512, 128, 4, n).transpose(0, 1, 3, 2))
    if fmt == "e4m3":
        words = by_word.astype(ml_dtypes.float8_e4m3fn).view(np.uint8)
    else:
        c = by_word.astype(ml_dtypes.float4_e2m1fn).view(np.uint8) & 0xF
        words = c[..., 0::2] | (c[..., 1::2] << 4)
    return np.ascontiguousarray(words), np.ascontiguousarray(byte.astype(np.uint8).reshape(k // 512, 16, n))


def unpack_weight(words, scales, fmt):
    g, p, n, _ = words.shape
    if fmt == "e4m3":
        vals = np.ascontiguousarray(words).view(ml_dtypes.float8_e4m3fn).astype(np.float64)
    else:
        nib = np.empty((g, p, n, 4), np.uint8)
        nib[..., 0::2] = words & 0xF
        nib[..., 1::2] = words >> 4
        vals = E2M1[nib]
    vals = vals * np.repeat(np.exp2(scales.astype(np.float64) - 127.0), 8, axis=1)[..., None]
    return vals.transpose(0, 1, 3, 2).reshape(g * 512, n)


B, S, D, H, KV, HD = 2, 256, 2048, 16, 8, 128
HALF = HD // 2
ROPE_BASE = 1.0e4
FMT = "e4m3"


def rotate_half(t):
    return np.concatenate((-t[..., HALF:], t[..., :HALF]), axis=-1)


def setup_inputs():
    s = mx_kscale(D)
    inv_freq = 1.0 / ROPE_BASE ** (np.arange(HALF) / HALF)
    freqs = np.outer(np.arange(S), inv_freq)
    emb = np.concatenate((freqs, freqs), axis=-1)
    w = 1.0 / np.sqrt(D)
    x = bf(np.random.standard_normal((B, S, D)) * s)
    Wq_words, Wq_scales = pack_weight(np.random.standard_normal((D, H * HD)) * w / s[:, None], FMT)
    Wk_words, Wk_scales = pack_weight(np.random.standard_normal((D, KV * HD)) * w / s[:, None], FMT)
    Wv_words, Wv_scales = pack_weight(np.random.standard_normal((D, KV * HD)) * w / s[:, None], FMT)
    return {"x": x,
            "cos": bf(np.cos(emb)),
            "sin": bf(np.sin(emb)),
            "Wq_words": Wq_words,
            "Wq_scales": Wq_scales,
            "Wk_words": Wk_words,
            "Wk_scales": Wk_scales,
            "Wv_words": Wv_words,
            "Wv_scales": Wv_scales}


def reference(x, cos, sin, Wq_words, Wq_scales, Wk_words, Wk_scales, Wv_words, Wv_scales):
    xq = mxq(f64(x), 2, "e4m3")
    q = (xq @ unpack_weight(Wq_words, Wq_scales, FMT)).reshape(B, S, H, HD)
    k = (xq @ unpack_weight(Wk_words, Wk_scales, FMT)).reshape(B, S, KV, HD)
    v = (xq @ unpack_weight(Wv_words, Wv_scales, FMT)).reshape(B, S, KV, HD)
    c = f64(cos)[None, :, None, :]
    sn = f64(sin)[None, :, None, :]
    q_rot = q * c + rotate_half(q) * sn
    k_rot = k * c + rotate_half(k) * sn
    return q_rot, k_rot, v

@@ -1,0 +1,195 @@
+from contextlib import ExitStack
+
+import concourse.mybir as mybir
+from concourse.masks import make_identity
+
+BF16 = mybir.dt.bfloat16
+F32 = mybir.dt.float32
+I32 = mybir.dt.int32
+U32 = mybir.dt.uint32
+U8 = mybir.dt.uint8
+FP8X4 = mybir.dt.float8_e4m3fn_x4
+MULT = mybir.AluOpType.mult
+ADD = mybir.AluOpType.add
+
+P = 128
+TOKENS = 512
+SEQ = 256
+D = 2048
+PACK = 4
+PASSES = D // (P * PACK)
+TOKEN_TILES = TOKENS // P
+HD = 128
+HALF = HD // 2
+BANK = 512
+BANK_HEADS = BANK // HD
+PSUM_BANKS = 8
+
+FLOPS = 2 * TOKENS * D * (2048 + 1024 + 1024)
+
+
+def tile_attention_pa_kernel(
+    tc, x, cos, sin, Wq_words, Wq_scales, Wk_words, Wk_scales, Wv_words, Wv_scales, out_0, out_1, out_2
+):
+    nc = tc.nc
+    x_rows = x.rearrange("b s d -> (b s) d")
+
+    weights = [
+        dict(name="q", words=Wq_words, scales=Wq_scales, out=out_0, cols=2048, plane_col=0, load_cols=BANK, rope=True),
+        dict(name="k", words=Wk_words, scales=Wk_scales, out=out_1, cols=1024, plane_col=2048, load_cols=1024, rope=True),
+        dict(name="v", words=Wv_words, scales=Wv_scales, out=out_2, cols=1024, plane_col=3072, load_cols=1024, rope=False),
+    ]
+    all_cols = sum(w["cols"] for w in weights)
+
+    with ExitStack() as ctx:
+        ctx.enter_context(tc.manual_schedule())
+        const = ctx.enter_context(tc.tile_pool(name="const", bufs=1))
+        x_pool = ctx.enter_context(tc.tile_pool(name="x", bufs=TOKEN_TILES))
+        w_pool = ctx.enter_context(tc.tile_pool(name="w", bufs=1))
+        out_pool = ctx.enter_context(tc.tile_pool(name="out", bufs=1))
+        psum = ctx.enter_context(tc.psum_pool(name="psum", bufs=PSUM_BANKS))
+
+        identity = const.tile([P, P], F32)
+        make_identity(nc, identity[:])
+
+        w_planes = const.tile([P, all_cols], U8, align_bytes=64)
+        nc.vector.memset(w_planes[:].bitcast(I32), 0)
+
+        def load_scales(w):
+            cols = slice(w["plane_col"], w["plane_col"] + w["cols"])
+            rows = w["scales"].bitcast(I32)
+            for quadrant in range(4):
+                nc.sync.dma_start(
+                    out=w_planes[32 * quadrant : 32 * quadrant + 16, cols].bitcast(I32),
+                    in_=rows[:, 4 * quadrant : 4 * quadrant + 4, :],
+                )
+
+        w_tiles = {}
+
+        def load_words(w, piece):
+            width = w["load_cols"]
+            words = w_pool.tile([P, PASSES, width], U32, name="w_%s%d" % (w["name"], piece), align_bytes=64)
+            view = w["words"].rearrange("g p n t -> p g (n t)").bitcast(I32)
+            nc.sync.dma_start(out=words[:].bitcast(I32), in_=view[:, :, piece * width : (piece + 1) * width])
+            w_tiles[(w["name"], piece)] = words
+
+        x_tiles = []
+
+        def load_x(m):
+            x_sb = x_pool.tile([P, D], BF16)
+            nc.sync.dma_start(out=x_sb[:], in_=x_rows[m * P : (m + 1) * P, :])
+            x_tiles.append(x_sb)
+
+        wq, wk, wv = weights
+        load_x(0)
+        load_scales(wq)
+        load_words(wq, 0)
+        for m in range(1, TOKEN_TILES):
+            load_x(m)
+        for piece in range(1, wq["cols"] // wq["load_cols"]):
+            load_words(wq, piece)
+        load_scales(wk)
+        load_scales(wv)
+        load_words(wk, 0)
+        load_words(wv, 0)
+
+        cos_sb = const.tile([P, SEQ // P, HD], BF16)
+        sin_sb = const.tile([P, SEQ // P, HD], BF16)
+        nc.scalar.dma_start(out=cos_sb[:], in_=cos.rearrange("(i p) d -> p i d", p=P))
+        nc.scalar.dma_start(out=sin_sb[:], in_=sin.rearrange("(i p) d -> p i d", p=P))
+        table = const.tile([P, SEQ // P, 2, HD], F32)
+        nc.gpsimd.tensor_copy(out=table[:, :, 0, :], in_=cos_sb[:])
+        nc.gpsimd.tensor_copy(out=table[:, :, 1, 0:HALF], in_=sin_sb[:, :, HALF:HD])
+        nc.gpsimd.tensor_scalar(
+            out=table[:, :, 1, HALF:HD], in0=sin_sb[:, :, 0:HALF], scalar1=-1.0, scalar2=None, op0=MULT
+        )
+
+        x_codes = []
+        x_scales = []
+
+        def quantise_x(m):
+            words = x_tiles[m][:].bitcast(F32)
+            grouped = x_pool.tile([P, PASSES, P, PACK], BF16, bufs=2, align_bytes=64)
+            grouped_words = grouped[:].bitcast(F32)
+            codes = x_pool.tile([P, PASSES, P], U32, align_bytes=64)
+            scales = x_pool.tile([P, PASSES, P], U8, align_bytes=64)
+            for pair in range(PASSES // 2):
+                turned = psum.tile([P, 2, 2, P], F32, tag="bank")
+                for i in range(2):
+                    first = (2 * pair + i) * 2 * P
+                    for u in range(2):
+                        nc.tensor.transpose(turned[:, i, u, :], words[:, first + u : first + 2 * P : 2], identity[:])
+                copy = nc.vector.tensor_copy if pair == 0 else nc.scalar.copy
+                copy(out=grouped_words[:, 2 * pair : 2 * pair + 2], in_=turned[:].rearrange("p g u t -> p g t u"))
+            for pair in range(PASSES // 2):
+                both = slice(2 * pair, 2 * pair + 2)
+                nc.vector.quantize_mx(
+                    out=codes[:, both, :].rearrange("p g t -> p (g t)").bitcast(FP8X4),
+                    scales=scales[:, both, :].rearrange("p g t -> p (g t)"),
+                    in_=grouped[:, both].rearrange("p g t c -> p (g t c)"),
+                )
+            x_codes.append(codes)
+            x_scales.append(scales)
+
+        def project(w, chunk, m):
+            bank = psum.tile([P, BANK], F32, tag="bank")
+            piece, col = divmod(chunk * BANK, w["load_cols"])
+            words = w_tiles[(w["name"], piece)]
+            plane_col = w["plane_col"] + chunk * BANK
+            for g in range(PASSES):
+                nc.tensor.matmul_mx(
+                    out=bank[:],
+                    lhsT=x_codes[m][:, g, :].bitcast(FP8X4),
+                    lhsT_scale=x_scales[m][:, g, :],
+                    rhs=words[:, g, col : col + BANK].bitcast(FP8X4),
+                    rhs_scale=w_planes[4 * g : P, plane_col : plane_col + BANK],
+                    start=(g == 0),
+                    stop=(g == PASSES - 1),
+                )
+            return bank
+
+        products = {}
+
+        def rope(w, chunk, m, bank):
+            if chunk == 0:
+                terms = out_pool.tile([P, 2, w["cols"]], F32, name="terms_%s%d" % (w["name"], m))
+                products[(w["name"], m)] = terms
+            terms = products[(w["name"], m)]
+            shape = [P, 2, BANK_HEADS, HD]
+            nc.vector.tensor_tensor(
+                out=terms[:, :, chunk * BANK : (chunk + 1) * BANK].rearrange("p r (h d) -> p r h d", d=HD),
+                in0=bank[:].rearrange("p (h d) -> p h d", d=HD).unsqueeze(1).to_broadcast(shape),
+                in1=table[:, m % 2].unsqueeze(2).to_broadcast(shape),
+                op=MULT,
+            )
+            if chunk % 2 == 1:
+                heads = slice((chunk - 1) * BANK_HEADS, (chunk + 1) * BANK_HEADS)
+                halves = terms[:].rearrange("p r (h s j) -> p r h s j", s=2, j=HALF)
+                for s in range(2):
+                    nc.gpsimd.tensor_tensor(
+                        out=halves[:, 0, heads, s, :],
+                        in0=halves[:, 0, heads, s, :],
+                        in1=halves[:, 1, heads, 1 - s, :],
+                        op=ADD,
+                    )
+            if (chunk + 1) * BANK == w["cols"]:
+                rows = w["out"].rearrange("b s h d -> (b s) (h d)")[m * P : (m + 1) * P, :]
+                nc.sync.dma_start(out=rows, in_=terms[:, 0, :])
+
+        def plain(w, chunk, m, bank):
+            copied = out_pool.tile([P, BANK], F32, name="copied_%d_%d" % (chunk, m))
+            nc.scalar.copy(out=copied[:], in_=bank[:])
+            rows = w["out"].rearrange("b s h d -> (b s) (h d)")[m * P : (m + 1) * P, :]
+            nc.scalar.dma_start(out=rows[:, chunk * BANK : (chunk + 1) * BANK], in_=copied[:])
+
+        quantise_x(0)
+        for w in weights:
+            for chunk in range(w["cols"] // BANK):
+                for m in range(TOKEN_TILES):
+                    bank = project(w, chunk, m)
+                    if len(x_codes) < TOKEN_TILES:
+                        quantise_x(len(x_codes))
+                    if w["rope"]:
+                        rope(w, chunk, m, bank)
+                    else:
+                        plain(w, chunk, m, bank)

@@ -34,28 +34,30 @@ def tile_attention_pa_kernel(
     nc = tc.nc
     x_rows = x.rearrange("b s d -> (b s) d")
 
-    weights = [
-        dict(name="q", words=Wq_words, scales=Wq_scales, out=out_0, cols=2048, plane_col=0, load_cols=BANK, rope=True),
-        dict(name="k", words=Wk_words, scales=Wk_scales, out=out_1, cols=1024, plane_col=2048, load_cols=1024, rope=True),
-        dict(name="v", words=Wv_words, scales=Wv_scales, out=out_2, cols=1024, plane_col=3072, load_cols=1024, rope=False),
-    ]
-    all_cols = sum(w["cols"] for w in weights)
+    weights = {
+        "q": dict(words=Wq_words, scales=Wq_scales, out=out_0, cols=2048, plane_col=0),
+        "k": dict(words=Wk_words, scales=Wk_scales, out=out_1, cols=1024, plane_col=2048),
+        "v": dict(words=Wv_words, scales=Wv_scales, out=out_2, cols=1024, plane_col=3072),
+    }
+    all_cols = 4096
 
     with ExitStack() as ctx:
         ctx.enter_context(tc.manual_schedule())
         const = ctx.enter_context(tc.tile_pool(name="const", bufs=1))
         x_pool = ctx.enter_context(tc.tile_pool(name="x", bufs=TOKEN_TILES))
         w_pool = ctx.enter_context(tc.tile_pool(name="w", bufs=1))
+        terms_pool = ctx.enter_context(tc.tile_pool(name="terms", bufs=4))
         out_pool = ctx.enter_context(tc.tile_pool(name="out", bufs=1))
         psum = ctx.enter_context(tc.psum_pool(name="psum", bufs=PSUM_BANKS))
-
-        identity = const.tile([P, P], F32)
-        make_identity(nc, identity[:])
 
         w_planes = const.tile([P, all_cols], U8, align_bytes=64)
         nc.vector.memset(w_planes[:].bitcast(I32), 0)
 
-        def load_scales(w):
+        identity = const.tile([P, P], F32)
+        make_identity(nc, identity[:])
+
+        def load_scales(name):
+            w = weights[name]
             cols = slice(w["plane_col"], w["plane_col"] + w["cols"])
             rows = w["scales"].bitcast(I32)
             for quadrant in range(4):
@@ -64,55 +66,67 @@ def tile_attention_pa_kernel(
                     in_=rows[:, 4 * quadrant : 4 * quadrant + 4, :],
                 )
 
-        w_tiles = {}
+        pieces = []
 
-        def load_words(w, piece):
-            width = w["load_cols"]
-            words = w_pool.tile([P, PASSES, width], U32, name="w_%s%d" % (w["name"], piece), align_bytes=64)
-            view = w["words"].rearrange("g p n t -> p g (n t)").bitcast(I32)
-            nc.sync.dma_start(out=words[:].bitcast(I32), in_=view[:, :, piece * width : (piece + 1) * width])
-            w_tiles[(w["name"], piece)] = words
+        def load_words(name, first, width):
+            words = w_pool.tile([P, PASSES, width], U32, name="w_%s%d" % (name, first), align_bytes=64)
+            view = weights[name]["words"].rearrange("g p n t -> p g (n t)").bitcast(I32)
+            nc.sync.dma_start(out=words[:].bitcast(I32), in_=view[:, :, first : first + width])
+            pieces.append((name, first, width, words))
+
+        def moving(name, col, n, g):
+            for piece_name, first, width, words in pieces:
+                if piece_name == name and first <= col and col + n <= first + width:
+                    return words[:, g, col - first : col - first + n]
+            return None
 
         x_tiles = []
-
-        def load_x(m):
+        for m in range(TOKEN_TILES):
             x_sb = x_pool.tile([P, D], BF16)
             nc.sync.dma_start(out=x_sb[:], in_=x_rows[m * P : (m + 1) * P, :])
             x_tiles.append(x_sb)
-
-        wq, wk, wv = weights
-        load_x(0)
-        load_scales(wq)
-        load_words(wq, 0)
-        for m in range(1, TOKEN_TILES):
-            load_x(m)
-        for piece in range(1, wq["cols"] // wq["load_cols"]):
-            load_words(wq, piece)
-        load_scales(wk)
-        load_scales(wv)
-        load_words(wk, 0)
-        load_words(wv, 0)
+        load_scales("q")
+        load_words("q", 0, 256)
+        load_words("q", 256, 256)
+        load_words("q", 512, 512)
+        load_words("q", 1024, 1024)
+        load_scales("v")
+        load_scales("k")
+        load_words("v", 0, 1024)
+        load_words("k", 0, 1024)
 
         cos_sb = const.tile([P, SEQ // P, HD], BF16)
         sin_sb = const.tile([P, SEQ // P, HD], BF16)
         nc.scalar.dma_start(out=cos_sb[:], in_=cos.rearrange("(i p) d -> p i d", p=P))
         nc.scalar.dma_start(out=sin_sb[:], in_=sin.rearrange("(i p) d -> p i d", p=P))
-        table = const.tile([P, SEQ // P, 2, HD], F32)
-        nc.gpsimd.tensor_copy(out=table[:, :, 0, :], in_=cos_sb[:])
-        nc.gpsimd.tensor_copy(out=table[:, :, 1, 0:HALF], in_=sin_sb[:, :, HALF:HD])
+        warm = const.tile([P, 1], F32)
+        nc.scalar.copy(out=warm[:], in_=identity[:, 0:1])
+        small = const.tile([P, SEQ // P, 4, HALF], F32)
         nc.gpsimd.tensor_scalar(
-            out=table[:, :, 1, HALF:HD], in0=sin_sb[:, :, 0:HALF], scalar1=-1.0, scalar2=None, op0=MULT
+            out=small[:, :, 0:4:3, :], in0=cos_sb[:].rearrange("p i (e j) -> p i e j", j=HALF),
+            scalar1=1.0, scalar2=0.0, op0=MULT, op1=ADD,
+        )
+        nc.gpsimd.tensor_scalar(
+            out=small[:, :, 1, :], in0=sin_sb[:, :, HALF:HD], scalar1=1.0, scalar2=0.0, op0=MULT, op1=ADD
+        )
+        nc.gpsimd.tensor_scalar(
+            out=small[:, :, 2, :], in0=sin_sb[:, :, 0:HALF], scalar1=-1.0, scalar2=0.0, op0=MULT, op1=ADD
+        )
+        table = const.tile([P, SEQ // P, BANK_HEADS, 4 * HALF], F32)
+        nc.gpsimd.tensor_scalar(
+            out=table[:],
+            in0=small[:].rearrange("p i c j -> p i (c j)").unsqueeze(2).to_broadcast([P, SEQ // P, BANK_HEADS, 4 * HALF]),
+            scalar1=1.0, scalar2=0.0, op0=MULT, op1=ADD,
         )
 
+        grouped_tiles = []
         x_codes = []
         x_scales = []
 
-        def quantise_x(m):
+        def turn(m):
             words = x_tiles[m][:].bitcast(F32)
-            grouped = x_pool.tile([P, PASSES, P, PACK], BF16, bufs=2, align_bytes=64)
+            grouped = x_pool.tile([P, PASSES, P, PACK], BF16, align_bytes=64)
             grouped_words = grouped[:].bitcast(F32)
-            codes = x_pool.tile([P, PASSES, P], U32, align_bytes=64)
-            scales = x_pool.tile([P, PASSES, P], U8, align_bytes=64)
             for pair in range(PASSES // 2):
                 turned = psum.tile([P, 2, 2, P], F32, tag="bank")
                 for i in range(2):
@@ -121,75 +135,124 @@ def tile_attention_pa_kernel(
                         nc.tensor.transpose(turned[:, i, u, :], words[:, first + u : first + 2 * P : 2], identity[:])
                 copy = nc.vector.tensor_copy if pair == 0 else nc.scalar.copy
                 copy(out=grouped_words[:, 2 * pair : 2 * pair + 2], in_=turned[:].rearrange("p g u t -> p g t u"))
-            for pair in range(PASSES // 2):
-                both = slice(2 * pair, 2 * pair + 2)
-                nc.vector.quantize_mx(
-                    out=codes[:, both, :].rearrange("p g t -> p (g t)").bitcast(FP8X4),
-                    scales=scales[:, both, :].rearrange("p g t -> p (g t)"),
-                    in_=grouped[:, both].rearrange("p g t c -> p (g t c)"),
-                )
+            grouped_tiles.append(grouped)
+
+        def quantise(m):
+            codes = x_pool.tile([P, PASSES, P], U32, align_bytes=64)
+            scales = x_pool.tile([P, PASSES, P], U8, align_bytes=64)
+            nc.vector.quantize_mx(
+                out=codes[:].rearrange("p g t -> p (g t)").bitcast(FP8X4),
+                scales=scales[:].rearrange("p g t -> p (g t)"),
+                in_=grouped_tiles[m][:].rearrange("p g t c -> p (g t c)"),
+            )
             x_codes.append(codes)
             x_scales.append(scales)
 
-        def project(w, chunk, m):
-            bank = psum.tile([P, BANK], F32, tag="bank")
-            piece, col = divmod(chunk * BANK, w["load_cols"])
-            words = w_tiles[(w["name"], piece)]
-            plane_col = w["plane_col"] + chunk * BANK
+        turn(0)
+        for m in range(1, TOKEN_TILES):
+            turn(m)
+            quantise(m - 1)
+        quantise(TOKEN_TILES - 1)
+
+        def project(name, col, n, m, out_ap):
+            plane_col = weights[name]["plane_col"] + col
             for g in range(PASSES):
                 nc.tensor.matmul_mx(
-                    out=bank[:],
+                    out=out_ap,
                     lhsT=x_codes[m][:, g, :].bitcast(FP8X4),
                     lhsT_scale=x_scales[m][:, g, :],
-                    rhs=words[:, g, col : col + BANK].bitcast(FP8X4),
-                    rhs_scale=w_planes[4 * g : P, plane_col : plane_col + BANK],
+                    rhs=moving(name, col, n, g).bitcast(FP8X4),
+                    rhs_scale=w_planes[4 * g : P, plane_col : plane_col + n],
                     start=(g == 0),
                     stop=(g == PASSES - 1),
                 )
-            return bank
 
-        products = {}
-
-        def rope(w, chunk, m, bank):
-            if chunk == 0:
-                terms = out_pool.tile([P, 2, w["cols"]], F32, name="terms_%s%d" % (w["name"], m))
-                products[(w["name"], m)] = terms
-            terms = products[(w["name"], m)]
-            shape = [P, 2, BANK_HEADS, HD]
+        def products(bank, m, terms_ap):
+            shape = [P, 2 * BANK_HEADS, 2, HALF]
             nc.vector.tensor_tensor(
-                out=terms[:, :, chunk * BANK : (chunk + 1) * BANK].rearrange("p r (h d) -> p r h d", d=HD),
-                in0=bank[:].rearrange("p (h d) -> p h d", d=HD).unsqueeze(1).to_broadcast(shape),
-                in1=table[:, m % 2].unsqueeze(2).to_broadcast(shape),
+                out=terms_ap.rearrange("p (c o j) -> p c o j", o=2, j=HALF),
+                in0=bank[:].rearrange("p (c j) -> p c j", j=HALF).unsqueeze(2).to_broadcast(shape),
+                in1=table[:, m % 2].rearrange("p h (s o j) -> p (h s) o j", o=2, j=HALF),
                 op=MULT,
             )
-            if chunk % 2 == 1:
-                heads = slice((chunk - 1) * BANK_HEADS, (chunk + 1) * BANK_HEADS)
-                halves = terms[:].rearrange("p r (h s j) -> p r h s j", s=2, j=HALF)
-                for s in range(2):
-                    nc.gpsimd.tensor_tensor(
-                        out=halves[:, 0, heads, s, :],
-                        in0=halves[:, 0, heads, s, :],
-                        in1=halves[:, 1, heads, 1 - s, :],
-                        op=ADD,
-                    )
-            if (chunk + 1) * BANK == w["cols"]:
-                rows = w["out"].rearrange("b s h d -> (b s) (h d)")[m * P : (m + 1) * P, :]
-                nc.sync.dma_start(out=rows, in_=terms[:, 0, :])
 
-        def plain(w, chunk, m, bank):
-            copied = out_pool.tile([P, BANK], F32, name="copied_%d_%d" % (chunk, m))
-            nc.scalar.copy(out=copied[:], in_=bank[:])
-            rows = w["out"].rearrange("b s h d -> (b s) (h d)")[m * P : (m + 1) * P, :]
-            nc.scalar.dma_start(out=rows[:, chunk * BANK : (chunk + 1) * BANK], in_=copied[:])
+        def add_terms(terms, result):
+            both = terms[:].rearrange("p b (h s d) -> p (b h) s d", s=2, d=HD)
+            nc.gpsimd.tensor_tensor(
+                out=result[:].rearrange("p b (h d) -> p (b h) d", d=HD), in0=both[:, :, 0, :], in1=both[:, :, 1, :], op=ADD
+            )
 
-        quantise_x(0)
-        for w in weights:
-            for chunk in range(w["cols"] // BANK):
-                for m in range(TOKEN_TILES):
-                    bank = project(w, chunk, m)
-                    if len(x_codes) < TOKEN_TILES:
-                        quantise_x(len(x_codes))
-                    if w["rope"]:
-                        rope(w, chunk, m, bank)
-                    else:
-                        plain(w, chunk, m, bank)
+        def out_rows(name):
+            return weights[name]["out"].rearrange("b s h d -> (b s) (h d)")
+
+        count = [0]
+
+        def new_pair():
+            count[0] += 1
+            terms = terms_pool.tile([P, 2, 2 * BANK], F32, name="terms")
+            result = out_pool.tile([P, 2, BANK], F32, name="result_%d" % count[0])
+            return terms, result
+
+        def finish_tiles_pair(col, m0, banks):
+            terms, result = new_pair()
+            for i in range(2):
+                products(banks[i], m0 + i, terms[:, i, :])
+            add_terms(terms, result)
+            rows = out_rows("q").rearrange("(m p) c -> p m c", p=P)
+            nc.sync.dma_start(out=rows[:, m0 : m0 + 2, col : col + BANK], in_=result[:])
+
+        for m0 in (0, 2):
+            pair_banks = []
+            for i in range(2):
+                bank = psum.tile([P, BANK], F32, tag="bank")
+                pair_banks.append(bank)
+            if m0 == 0:
+                for half in range(2):
+                    for i in range(2):
+                        project("q", 256 * half, 256, m0 + i, pair_banks[i][:, 256 * half : 256 * half + 256])
+            else:
+                for i in range(2):
+                    for half in range(2):
+                        project("q", 256 * half, 256, m0 + i, pair_banks[i][:, 256 * half : 256 * half + 256])
+            finish_tiles_pair(0, m0, pair_banks)
+        for m0 in (0, 2):
+            pair_banks = []
+            for i in range(2):
+                bank = psum.tile([P, BANK], F32, tag="bank")
+                project("q", BANK, BANK, m0 + i, bank[:])
+                pair_banks.append(bank)
+            finish_tiles_pair(BANK, m0, pair_banks)
+
+        def rope_unit(name, col, m):
+            terms, result = new_pair()
+            for i in range(2):
+                bank = psum.tile([P, BANK], F32, tag="bank")
+                project(name, col + i * BANK, BANK, m, bank[:])
+                products(bank, m, terms[:, i, :])
+            add_terms(terms, result)
+            nc.sync.dma_start(
+                out=out_rows(name)[m * P : (m + 1) * P, col : col + 2 * BANK], in_=result[:].rearrange("p b c -> p (b c)")
+            )
+
+        def plain_unit(name, col, m, together):
+            copied = out_pool.tile([P, 2, BANK], F32, name="copied_%d" % m)
+            rows = out_rows(name)[m * P : (m + 1) * P, :]
+            for i in range(2):
+                bank = psum.tile([P, BANK], F32, tag="bank")
+                project(name, col + i * BANK, BANK, m, bank[:])
+                nc.scalar.copy(out=copied[:, i, :], in_=bank[:])
+                if not together:
+                    nc.scalar.dma_start(out=rows[:, col + i * BANK : col + (i + 1) * BANK], in_=copied[:, i, :])
+            if together:
+                nc.scalar.dma_start(out=rows[:, col : col + 2 * BANK], in_=copied[:].rearrange("p b c -> p (b c)"))
+
+        for m in range(TOKEN_TILES):
+            rope_unit("q", 1024, m)
+        plain_unit("v", 0, 0, True)
+        rope_unit("k", 0, 0)
+        rope_unit("k", 0, 1)
+        plain_unit("v", 0, 1, True)
+        rope_unit("k", 0, 2)
+        rope_unit("k", 0, 3)
+        plain_unit("v", 0, 2, True)
+        plain_unit("v", 0, 3, False)

@@ -50,11 +50,18 @@ def tile_attention_pa_kernel(
         out_pool = ctx.enter_context(tc.tile_pool(name="out", bufs=1))
         psum = ctx.enter_context(tc.psum_pool(name="psum", bufs=PSUM_BANKS))
 
+        zeros = const.tile([P, BANK], BF16)
+        nc.vector.memset(zeros[:], 0.0)
+
         w_planes = const.tile([P, all_cols], U8, align_bytes=64)
         nc.vector.memset(w_planes[:].bitcast(I32), 0)
 
         identity = const.tile([P, P], F32)
         make_identity(nc, identity[:])
+
+        def idle_matmuls(bank_ap, n):
+            for i in range(n):
+                nc.tensor.matmul(out=bank_ap, lhsT=zeros[:, 0:P], rhs=zeros[:], start=True, stop=True)
 
         def load_scales(name):
             w = weights[name]
@@ -123,12 +130,14 @@ def tile_attention_pa_kernel(
         x_codes = []
         x_scales = []
 
-        def turn(m):
+        def turn(m, idle):
             words = x_tiles[m][:].bitcast(F32)
             grouped = x_pool.tile([P, PASSES, P, PACK], BF16, align_bytes=64)
             grouped_words = grouped[:].bitcast(F32)
             for pair in range(PASSES // 2):
                 turned = psum.tile([P, 2, 2, P], F32, tag="bank")
+                if pair == 0:
+                    idle_matmuls(turned[:].rearrange("p g u t -> p (g u t)"), idle)
                 for i in range(2):
                     first = (2 * pair + i) * 2 * P
                     for u in range(2):
@@ -148,9 +157,9 @@ def tile_attention_pa_kernel(
             x_codes.append(codes)
             x_scales.append(scales)
 
-        turn(0)
+        turn(0, 6)
         for m in range(1, TOKEN_TILES):
-            turn(m)
+            turn(m, 2)
             quantise(m - 1)
         quantise(TOKEN_TILES - 1)
 
@@ -207,6 +216,7 @@ def tile_attention_pa_kernel(
                 bank = psum.tile([P, BANK], F32, tag="bank")
                 pair_banks.append(bank)
             if m0 == 0:
+                idle_matmuls(pair_banks[0][:], 2)
                 for half in range(2):
                     for i in range(2):
                         project("q", 256 * half, 256, m0 + i, pair_banks[i][:, 256 * half : 256 * half + 256])

@@ -63,14 +63,14 @@ def tile_attention_pa_kernel(
             for i in range(n):
                 nc.tensor.matmul(out=bank_ap, lhsT=zeros[:, 0:P], rhs=zeros[:], start=True, stop=True)
 
-        def load_scales(name):
+        def load_scales(name, first, width):
             w = weights[name]
-            cols = slice(w["plane_col"], w["plane_col"] + w["cols"])
+            cols = slice(w["plane_col"] + first, w["plane_col"] + first + width)
             rows = w["scales"].bitcast(I32)
             for quadrant in range(4):
                 nc.sync.dma_start(
                     out=w_planes[32 * quadrant : 32 * quadrant + 16, cols].bitcast(I32),
-                    in_=rows[:, 4 * quadrant : 4 * quadrant + 4, :],
+                    in_=rows[:, 4 * quadrant : 4 * quadrant + 4, first // 4 : (first + width) // 4],
                 )
 
         pieces = []
@@ -92,46 +92,54 @@ def tile_attention_pa_kernel(
             x_sb = x_pool.tile([P, D], BF16)
             nc.sync.dma_start(out=x_sb[:], in_=x_rows[m * P : (m + 1) * P, :])
             x_tiles.append(x_sb)
-        load_scales("q")
-        load_words("q", 0, 256)
-        load_words("q", 256, 256)
-        load_words("q", 512, 512)
-        load_words("q", 1024, 1024)
-        load_scales("v")
-        load_scales("k")
-        load_words("v", 0, 1024)
-        load_words("k", 0, 1024)
-
         cos_sb = const.tile([P, SEQ // P, HD], BF16)
         sin_sb = const.tile([P, SEQ // P, HD], BF16)
-        nc.scalar.dma_start(out=cos_sb[:], in_=cos.rearrange("(i p) d -> p i d", p=P))
-        nc.scalar.dma_start(out=sin_sb[:], in_=sin.rearrange("(i p) d -> p i d", p=P))
+        load_scales("q", 0, 512)
+        load_words("q", 0, 256)
+        nc.sync.dma_start(out=cos_sb[:], in_=cos.rearrange("(i p) d -> p i d", p=P))
+        nc.sync.dma_start(out=sin_sb[:], in_=sin.rearrange("(i p) d -> p i d", p=P))
+        load_words("q", 256, 256)
+        load_scales("q", 512, 512)
+        load_words("q", 512, 512)
+        load_scales("q", 1024, 1024)
+        load_words("q", 1024, 512)
+        load_words("q", 1536, 512)
+        load_scales("k", 0, 1024)
+        load_scales("v", 0, 1024)
+        load_words("k", 0, 1024)
+        load_words("v", 0, 1024)
+
         warm = const.tile([P, 1], F32)
         nc.scalar.copy(out=warm[:], in_=identity[:, 0:1])
-        small = const.tile([P, SEQ // P, 4, HALF], F32)
-        nc.gpsimd.tensor_scalar(
-            out=small[:, :, 0:4:3, :], in0=cos_sb[:].rearrange("p i (e j) -> p i e j", j=HALF),
-            scalar1=1.0, scalar2=0.0, op0=MULT, op1=ADD,
-        )
-        nc.gpsimd.tensor_scalar(
-            out=small[:, :, 1, :], in0=sin_sb[:, :, HALF:HD], scalar1=1.0, scalar2=0.0, op0=MULT, op1=ADD
-        )
-        nc.gpsimd.tensor_scalar(
-            out=small[:, :, 2, :], in0=sin_sb[:, :, 0:HALF], scalar1=-1.0, scalar2=0.0, op0=MULT, op1=ADD
-        )
-        table = const.tile([P, SEQ // P, BANK_HEADS, 4 * HALF], F32)
-        nc.gpsimd.tensor_scalar(
-            out=table[:],
-            in0=small[:].rearrange("p i c j -> p i (c j)").unsqueeze(2).to_broadcast([P, SEQ // P, BANK_HEADS, 4 * HALF]),
-            scalar1=1.0, scalar2=0.0, op0=MULT, op1=ADD,
-        )
+        table = const.tile([P, SEQ // P, BANK_HEADS, 4, HALF], F32)
+        for i in range(SEQ // P):
+            nc.gpsimd.tensor_scalar(
+                out=table[:, i, :, 0:4:3, :],
+                in0=cos_sb[:, i].rearrange("p (e j) -> p e j", j=HALF).unsqueeze(1).to_broadcast([P, BANK_HEADS, 2, HALF]),
+                scalar1=1.0, scalar2=0.0, op0=MULT, op1=ADD,
+            )
+            nc.gpsimd.tensor_scalar(
+                out=table[:, i, :, 1, :], in0=sin_sb[:, i, HALF:HD].unsqueeze(1).to_broadcast([P, BANK_HEADS, HALF]),
+                scalar1=1.0, scalar2=0.0, op0=MULT, op1=ADD,
+            )
+            nc.gpsimd.tensor_scalar(
+                out=table[:, i, :, 2, :], in0=sin_sb[:, i, 0:HALF].unsqueeze(1).to_broadcast([P, BANK_HEADS, HALF]),
+                scalar1=-1.0, scalar2=0.0, op0=MULT, op1=ADD,
+            )
 
         grouped_tiles = []
         x_codes = []
         x_scales = []
 
-        def turn(m, idle):
+        sorted_tiles = []
+
+        def sort_words(m):
             words = x_tiles[m][:].bitcast(F32)
+            sorted_words = x_pool.tile([P, PASSES, 2, P], F32, bufs=2)
+            nc.vector.tensor_copy(out=sorted_words[:], in_=words.rearrange("t (g p u) -> t g u p", g=PASSES, u=2))
+            sorted_tiles.append(sorted_words)
+
+        def turn(m, idle):
             grouped = x_pool.tile([P, PASSES, P, PACK], BF16, align_bytes=64)
             grouped_words = grouped[:].bitcast(F32)
             for pair in range(PASSES // 2):
@@ -139,11 +147,9 @@ def tile_attention_pa_kernel(
                 if pair == 0:
                     idle_matmuls(turned[:].rearrange("p g u t -> p (g u t)"), idle)
                 for i in range(2):
-                    first = (2 * pair + i) * 2 * P
                     for u in range(2):
-                        nc.tensor.transpose(turned[:, i, u, :], words[:, first + u : first + 2 * P : 2], identity[:])
-                copy = nc.vector.tensor_copy if pair == 0 else nc.scalar.copy
-                copy(out=grouped_words[:, 2 * pair : 2 * pair + 2], in_=turned[:].rearrange("p g u t -> p g t u"))
+                        nc.tensor.transpose(turned[:, i, u, :], sorted_tiles[m][:, 2 * pair + i, u, :], identity[:])
+                nc.scalar.copy(out=grouped_words[:, 2 * pair : 2 * pair + 2], in_=turned[:].rearrange("p g u t -> p g t u"))
             grouped_tiles.append(grouped)
 
         def quantise(m):
@@ -157,11 +163,18 @@ def tile_attention_pa_kernel(
             x_codes.append(codes)
             x_scales.append(scales)
 
-        turn(0, 6)
-        for m in range(1, TOKEN_TILES):
-            turn(m, 2)
-            quantise(m - 1)
-        quantise(TOKEN_TILES - 1)
+        sort_words(0)
+        turn(0, 8)
+        sort_words(1)
+        turn(1, 2)
+        sort_words(2)
+        quantise(0)
+        turn(2, 2)
+        sort_words(3)
+        quantise(1)
+        turn(3, 2)
+        quantise(2)
+        quantise(3)
 
         def project(name, col, n, m, out_ap):
             plane_col = weights[name]["plane_col"] + col
@@ -181,7 +194,7 @@ def tile_attention_pa_kernel(
             nc.vector.tensor_tensor(
                 out=terms_ap.rearrange("p (c o j) -> p c o j", o=2, j=HALF),
                 in0=bank[:].rearrange("p (c j) -> p c j", j=HALF).unsqueeze(2).to_broadcast(shape),
-                in1=table[:, m % 2].rearrange("p h (s o j) -> p (h s) o j", o=2, j=HALF),
+                in1=table[:, m % 2].rearrange("p h (s o) j -> p (h s) o j", o=2),
                 op=MULT,
             )
 
@@ -210,28 +223,24 @@ def tile_attention_pa_kernel(
             rows = out_rows("q").rearrange("(m p) c -> p m c", p=P)
             nc.sync.dma_start(out=rows[:, m0 : m0 + 2, col : col + BANK], in_=result[:])
 
+        first_banks = []
+        for m in range(TOKEN_TILES):
+            bank = psum.tile([P, BANK], F32, tag="bank")
+            first_banks.append(bank)
+        idle_matmuls(first_banks[0][:], 2)
+        for half in range(2):
+            for m in range(TOKEN_TILES):
+                project("q", 256 * half, 256, m, first_banks[m][:, 256 * half : 256 * half + 256])
         for m0 in (0, 2):
-            pair_banks = []
-            for i in range(2):
-                bank = psum.tile([P, BANK], F32, tag="bank")
-                pair_banks.append(bank)
-            if m0 == 0:
-                idle_matmuls(pair_banks[0][:], 2)
-                for half in range(2):
-                    for i in range(2):
-                        project("q", 256 * half, 256, m0 + i, pair_banks[i][:, 256 * half : 256 * half + 256])
-            else:
+            finish_tiles_pair(0, m0, first_banks[m0 : m0 + 2])
+        for col in (BANK, 2 * BANK, 3 * BANK):
+            for m0 in (0, 2):
+                pair_banks = []
                 for i in range(2):
-                    for half in range(2):
-                        project("q", 256 * half, 256, m0 + i, pair_banks[i][:, 256 * half : 256 * half + 256])
-            finish_tiles_pair(0, m0, pair_banks)
-        for m0 in (0, 2):
-            pair_banks = []
-            for i in range(2):
-                bank = psum.tile([P, BANK], F32, tag="bank")
-                project("q", BANK, BANK, m0 + i, bank[:])
-                pair_banks.append(bank)
-            finish_tiles_pair(BANK, m0, pair_banks)
+                    bank = psum.tile([P, BANK], F32, tag="bank")
+                    project("q", col, BANK, m0 + i, bank[:])
+                    pair_banks.append(bank)
+                finish_tiles_pair(col, m0, pair_banks)
 
         def rope_unit(name, col, m):
             terms, result = new_pair()
@@ -256,13 +265,11 @@ def tile_attention_pa_kernel(
             if together:
                 nc.scalar.dma_start(out=rows[:, col : col + 2 * BANK], in_=copied[:].rearrange("p b c -> p (b c)"))
 
-        for m in range(TOKEN_TILES):
-            rope_unit("q", 1024, m)
-        plain_unit("v", 0, 0, True)
         rope_unit("k", 0, 0)
         rope_unit("k", 0, 1)
-        plain_unit("v", 0, 1, True)
+        plain_unit("v", 0, 0, True)
         rope_unit("k", 0, 2)
         rope_unit("k", 0, 3)
+        plain_unit("v", 0, 1, True)
         plain_unit("v", 0, 2, True)
         plain_unit("v", 0, 3, False)

@@ -53,7 +53,7 @@ def tile_attention_pa_kernel(
         zeros = const.tile([P, BANK], BF16)
         nc.vector.memset(zeros[:], 0.0)
 
-        w_planes = const.tile([P, all_cols], U8, align_bytes=64)
+        w_planes = const.tile([P, all_cols], U8, align_bytes=256)
         nc.vector.memset(w_planes[:].bitcast(I32), 0)
 
         identity = const.tile([P, P], F32)
@@ -76,7 +76,7 @@ def tile_attention_pa_kernel(
         pieces = []
 
         def load_words(name, first, width):
-            words = w_pool.tile([P, PASSES, width], U32, name="w_%s%d" % (name, first), align_bytes=64)
+            words = w_pool.tile([P, PASSES, width], U32, name="w_%s%d" % (name, first), align_bytes=256)
             view = weights[name]["words"].rearrange("g p n t -> p g (n t)").bitcast(I32)
             nc.sync.dma_start(out=words[:].bitcast(I32), in_=view[:, :, first : first + width])
             pieces.append((name, first, width, words))
@@ -140,7 +140,7 @@ def tile_attention_pa_kernel(
             sorted_tiles.append(sorted_words)
 
         def turn(m, idle):
-            grouped = x_pool.tile([P, PASSES, P, PACK], BF16, align_bytes=64)
+            grouped = x_pool.tile([P, PASSES, P, PACK], BF16, align_bytes=256)
             grouped_words = grouped[:].bitcast(F32)
             for pair in range(PASSES // 2):
                 turned = psum.tile([P, 2, 2, P], F32, tag="bank")
@@ -153,8 +153,8 @@ def tile_attention_pa_kernel(
             grouped_tiles.append(grouped)
 
         def quantise(m):
-            codes = x_pool.tile([P, PASSES, P], U32, align_bytes=64)
-            scales = x_pool.tile([P, PASSES, P], U8, align_bytes=64)
+            codes = x_pool.tile([P, PASSES, P], U32, align_bytes=256)
+            scales = x_pool.tile([P, PASSES, P], U8, align_bytes=256)
             nc.vector.quantize_mx(
                 out=codes[:].rearrange("p g t -> p (g t)").bitcast(FP8X4),
                 scales=scales[:].rearrange("p g t -> p (g t)"),

@@ -75,16 +75,21 @@ def tile_attention_pa_kernel(
 
         pieces = []
 
-        def load_words(name, first, width):
-            words = w_pool.tile([P, PASSES, width], U32, name="w_%s%d" % (name, first), align_bytes=256)
+        def load_words(name, first, width, first_pass=0, n_passes=PASSES):
+            words = w_pool.tile(
+                [P, n_passes, width], U32, name="w_%s%d_%d" % (name, first, first_pass), align_bytes=256
+            )
             view = weights[name]["words"].rearrange("g p n t -> p g (n t)").bitcast(I32)
-            nc.sync.dma_start(out=words[:].bitcast(I32), in_=view[:, :, first : first + width])
-            pieces.append((name, first, width, words))
+            nc.sync.dma_start(
+                out=words[:].bitcast(I32), in_=view[:, first_pass : first_pass + n_passes, first : first + width]
+            )
+            pieces.append((name, first, width, first_pass, n_passes, words))
 
         def moving(name, col, n, g):
-            for piece_name, first, width, words in pieces:
+            for piece_name, first, width, first_pass, n_passes, words in pieces:
                 if piece_name == name and first <= col and col + n <= first + width:
-                    return words[:, g, col - first : col - first + n]
+                    if first_pass <= g and g < first_pass + n_passes:
+                        return words[:, g - first_pass, col - first : col - first + n]
             return None
 
         x_tiles = []
@@ -95,12 +100,15 @@ def tile_attention_pa_kernel(
         cos_sb = const.tile([P, SEQ // P, HD], BF16)
         sin_sb = const.tile([P, SEQ // P, HD], BF16)
         load_scales("q", 0, 512)
-        load_words("q", 0, 256)
+        load_words("q", 0, BANK, 0, 1)
+        load_words("q", 0, BANK, 1, 1)
         nc.sync.dma_start(out=cos_sb[:], in_=cos.rearrange("(i p) d -> p i d", p=P))
         nc.sync.dma_start(out=sin_sb[:], in_=sin.rearrange("(i p) d -> p i d", p=P))
-        load_words("q", 256, 256)
+        load_words("q", 0, BANK, 2, 1)
+        load_words("q", 0, BANK, 3, 1)
         load_scales("q", 512, 512)
-        load_words("q", 512, 512)
+        load_words("q", 512, 512, 0, 2)
+        load_words("q", 512, 512, 2, 2)
         load_scales("q", 1024, 1024)
         load_words("q", 1024, 512)
         load_words("q", 1536, 512)
@@ -139,7 +147,8 @@ def tile_attention_pa_kernel(
             nc.vector.tensor_copy(out=sorted_words[:], in_=words.rearrange("t (g p u) -> t g u p", g=PASSES, u=2))
             sorted_tiles.append(sorted_words)
 
-        def turn(m, idle):
+        def turn(m, idle, is_sorted):
+            words = x_tiles[m][:].bitcast(F32)
             grouped = x_pool.tile([P, PASSES, P, PACK], BF16, align_bytes=256)
             grouped_words = grouped[:].bitcast(F32)
             for pair in range(PASSES // 2):
@@ -147,8 +156,13 @@ def tile_attention_pa_kernel(
                 if pair == 0:
                     idle_matmuls(turned[:].rearrange("p g u t -> p (g u t)"), idle)
                 for i in range(2):
+                    first = (2 * pair + i) * 2 * P
                     for u in range(2):
-                        nc.tensor.transpose(turned[:, i, u, :], sorted_tiles[m][:, 2 * pair + i, u, :], identity[:])
+                        if is_sorted:
+                            block = sorted_tiles[m][:, 2 * pair + i, u, :]
+                        else:
+                            block = words[:, first + u : first + 2 * P : 2]
+                        nc.tensor.transpose(turned[:, i, u, :], block, identity[:])
                 nc.scalar.copy(out=grouped_words[:, 2 * pair : 2 * pair + 2], in_=turned[:].rearrange("p g u t -> p g t u"))
             grouped_tiles.append(grouped)
 
@@ -164,30 +178,32 @@ def tile_attention_pa_kernel(
             x_scales.append(scales)
 
         sort_words(0)
-        turn(0, 8)
+        turn(0, 8, True)
         sort_words(1)
-        turn(1, 2)
+        turn(1, 2, True)
         sort_words(2)
         quantise(0)
-        turn(2, 2)
-        sort_words(3)
+        turn(2, 2, True)
         quantise(1)
-        turn(3, 2)
+        turn(3, 0, False)
         quantise(2)
         quantise(3)
 
-        def project(name, col, n, m, out_ap):
+        def one_pass(name, col, n, m, g, out_ap):
             plane_col = weights[name]["plane_col"] + col
+            nc.tensor.matmul_mx(
+                out=out_ap,
+                lhsT=x_codes[m][:, g, :].bitcast(FP8X4),
+                lhsT_scale=x_scales[m][:, g, :],
+                rhs=moving(name, col, n, g).bitcast(FP8X4),
+                rhs_scale=w_planes[4 * g : P, plane_col : plane_col + n],
+                start=(g == 0),
+                stop=(g == PASSES - 1),
+            )
+
+        def project(name, col, n, m, out_ap):
             for g in range(PASSES):
-                nc.tensor.matmul_mx(
-                    out=out_ap,
-                    lhsT=x_codes[m][:, g, :].bitcast(FP8X4),
-                    lhsT_scale=x_scales[m][:, g, :],
-                    rhs=moving(name, col, n, g).bitcast(FP8X4),
-                    rhs_scale=w_planes[4 * g : P, plane_col : plane_col + n],
-                    start=(g == 0),
-                    stop=(g == PASSES - 1),
-                )
+                one_pass(name, col, n, m, g, out_ap)
 
         def products(bank, m, terms_ap):
             shape = [P, 2 * BANK_HEADS, 2, HALF]
@@ -227,10 +243,11 @@ def tile_attention_pa_kernel(
         for m in range(TOKEN_TILES):
             bank = psum.tile([P, BANK], F32, tag="bank")
             first_banks.append(bank)
-        idle_matmuls(first_banks[0][:], 2)
-        for half in range(2):
-            for m in range(TOKEN_TILES):
-                project("q", 256 * half, 256, m, first_banks[m][:, 256 * half : 256 * half + 256])
+        stages = [((0, 1), (0, 1)), ((0, 1), (2,)), ((2, 3), (0, 1, 2)), ((0, 1, 2, 3), (3,))]
+        for stage_passes, stage_tiles in stages:
+            for g in stage_passes:
+                for m in stage_tiles:
+                    one_pass("q", 0, BANK, m, g, first_banks[m][:])
         for m0 in (0, 2):
             finish_tiles_pair(0, m0, first_banks[m0 : m0 + 2])
         for col in (BANK, 2 * BANK, 3 * BANK):

@@ -54,7 +54,8 @@ def tile_attention_pa_kernel(
         nc.vector.memset(zeros[:], 0.0)
 
         w_planes = const.tile([P, all_cols], U8, align_bytes=256)
-        nc.vector.memset(w_planes[:].bitcast(I32), 0)
+        nc.vector.memset(w_planes[:, 0:BANK].bitcast(I32), 0)
+        nc.vector.memset(w_planes[:, BANK:all_cols].bitcast(I32), 0)
 
         identity = const.tile([P, P], F32)
         make_identity(nc, identity[:])
@@ -93,26 +94,31 @@ def tile_attention_pa_kernel(
             return None
 
         x_tiles = []
-        for m in range(TOKEN_TILES):
+
+        def load_x(m):
             x_sb = x_pool.tile([P, D], BF16)
             nc.sync.dma_start(out=x_sb[:], in_=x_rows[m * P : (m + 1) * P, :])
             x_tiles.append(x_sb)
+
         cos_sb = const.tile([P, SEQ // P, HD], BF16)
         sin_sb = const.tile([P, SEQ // P, HD], BF16)
+        load_x(0)
+        load_x(1)
         load_scales("q", 0, 512)
+        load_x(2)
+        load_x(3)
         load_words("q", 0, BANK, 0, 1)
         load_words("q", 0, BANK, 1, 1)
         nc.sync.dma_start(out=cos_sb[:], in_=cos.rearrange("(i p) d -> p i d", p=P))
         nc.sync.dma_start(out=sin_sb[:], in_=sin.rearrange("(i p) d -> p i d", p=P))
         load_words("q", 0, BANK, 2, 1)
         load_words("q", 0, BANK, 3, 1)
-        load_scales("q", 512, 512)
         load_words("q", 512, 512, 0, 2)
+        load_scales("q", 512, 1536)
         load_words("q", 512, 512, 2, 2)
-        load_scales("q", 1024, 1024)
         load_words("q", 1024, 512)
-        load_words("q", 1536, 512)
         load_scales("k", 0, 1024)
+        load_words("q", 1536, 512)
         load_scales("v", 0, 1024)
         load_words("k", 0, 1024)
         load_words("v", 0, 1024)

@@ -104,15 +104,15 @@ def tile_attention_pa_kernel(
         sin_sb = const.tile([P, SEQ // P, HD], BF16)
         load_x(0)
         load_x(1)
-        load_scales("q", 0, 512)
         load_x(2)
         load_x(3)
+        load_scales("q", 0, 512)
         load_words("q", 0, BANK, 0, 1)
         load_words("q", 0, BANK, 1, 1)
-        nc.sync.dma_start(out=cos_sb[:], in_=cos.rearrange("(i p) d -> p i d", p=P))
-        nc.sync.dma_start(out=sin_sb[:], in_=sin.rearrange("(i p) d -> p i d", p=P))
         load_words("q", 0, BANK, 2, 1)
         load_words("q", 0, BANK, 3, 1)
+        nc.sync.dma_start(out=cos_sb[:], in_=cos.rearrange("(i p) d -> p i d", p=P))
+        nc.sync.dma_start(out=sin_sb[:], in_=sin.rearrange("(i p) d -> p i d", p=P))
         load_words("q", 512, 512, 0, 2)
         load_scales("q", 512, 1536)
         load_words("q", 512, 512, 2, 2)
@@ -220,9 +220,9 @@ def tile_attention_pa_kernel(
                 op=MULT,
             )
 
-        def add_terms(terms, result):
+        def add_terms(terms, result, engine):
             both = terms[:].rearrange("p b (h s d) -> p (b h) s d", s=2, d=HD)
-            nc.gpsimd.tensor_tensor(
+            engine.tensor_tensor(
                 out=result[:].rearrange("p b (h d) -> p (b h) d", d=HD), in0=both[:, :, 0, :], in1=both[:, :, 1, :], op=ADD
             )
 
@@ -241,7 +241,7 @@ def tile_attention_pa_kernel(
             terms, result = new_pair()
             for i in range(2):
                 products(banks[i], m0 + i, terms[:, i, :])
-            add_terms(terms, result)
+            add_terms(terms, result, nc.gpsimd)
             rows = out_rows("q").rearrange("(m p) c -> p m c", p=P)
             nc.sync.dma_start(out=rows[:, m0 : m0 + 2, col : col + BANK], in_=result[:])
 
@@ -265,34 +265,48 @@ def tile_attention_pa_kernel(
                     pair_banks.append(bank)
                 finish_tiles_pair(col, m0, pair_banks)
 
-        def rope_unit(name, col, m):
+        def rope_unit(name, col, m, add_engine):
             terms, result = new_pair()
             for i in range(2):
                 bank = psum.tile([P, BANK], F32, tag="bank")
                 project(name, col + i * BANK, BANK, m, bank[:])
                 products(bank, m, terms[:, i, :])
-            add_terms(terms, result)
+            add_terms(terms, result, add_engine)
             nc.sync.dma_start(
                 out=out_rows(name)[m * P : (m + 1) * P, col : col + 2 * BANK], in_=result[:].rearrange("p b c -> p (b c)")
             )
 
-        def plain_unit(name, col, m, together):
+        def copy_out(engine, out_ap, bank_ap):
+            if engine == "scalar":
+                nc.scalar.copy(out=out_ap, in_=bank_ap)
+            else:
+                nc.vector.tensor_copy(out=out_ap, in_=bank_ap)
+
+        def plain_unit(name, col, m):
             copied = out_pool.tile([P, 2, BANK], F32, name="copied_%d" % m)
-            rows = out_rows(name)[m * P : (m + 1) * P, :]
             for i in range(2):
                 bank = psum.tile([P, BANK], F32, tag="bank")
                 project(name, col + i * BANK, BANK, m, bank[:])
-                nc.scalar.copy(out=copied[:, i, :], in_=bank[:])
-                if not together:
-                    nc.scalar.dma_start(out=rows[:, col + i * BANK : col + (i + 1) * BANK], in_=copied[:, i, :])
-            if together:
-                nc.scalar.dma_start(out=rows[:, col : col + 2 * BANK], in_=copied[:].rearrange("p b c -> p (b c)"))
+                copy_out("scalar", copied[:, i, :], bank[:])
+            nc.scalar.dma_start(
+                out=out_rows(name)[m * P : (m + 1) * P, col : col + 2 * BANK], in_=copied[:].rearrange("p b c -> p (b c)")
+            )
 
-        rope_unit("k", 0, 0)
-        rope_unit("k", 0, 1)
-        plain_unit("v", 0, 0, True)
-        rope_unit("k", 0, 2)
-        rope_unit("k", 0, 3)
-        plain_unit("v", 0, 1, True)
-        plain_unit("v", 0, 2, True)
-        plain_unit("v", 0, 3, False)
+        def last_unit(name, m, widths):
+            first = 0
+            for i, (width, engine) in enumerate(widths):
+                copied = out_pool.tile([P, width], F32, name="last_%d" % i)
+                bank = psum.tile([P, BANK], F32, tag="bank")
+                project(name, first, width, m, bank[:, 0:width])
+                copy_out(engine, copied[:], bank[:, 0:width])
+                nc.sync.dma_start(out=out_rows(name)[m * P : (m + 1) * P, first : first + width], in_=copied[:])
+                first += width
+
+        rope_unit("k", 0, 0, nc.gpsimd)
+        rope_unit("k", 0, 1, nc.gpsimd)
+        plain_unit("v", 0, 0)
+        rope_unit("k", 0, 2, nc.gpsimd)
+        rope_unit("k", 0, 3, nc.vector)
+        plain_unit("v", 0, 1)
+        plain_unit("v", 0, 2)
+        last_unit("v", 3, [(512, "scalar"), (256, "vector"), (128, "scalar"), (128, "vector")])

@@ -109,10 +109,10 @@ def tile_attention_pa_kernel(
         load_scales("q", 0, 512)
         load_words("q", 0, BANK, 0, 1)
         load_words("q", 0, BANK, 1, 1)
+        nc.sync.dma_start(out=sin_sb[:], in_=sin.rearrange("(i p) d -> p i d", p=P))
+        nc.sync.dma_start(out=cos_sb[:], in_=cos.rearrange("(i p) d -> p i d", p=P))
         load_words("q", 0, BANK, 2, 1)
         load_words("q", 0, BANK, 3, 1)
-        nc.sync.dma_start(out=cos_sb[:], in_=cos.rearrange("(i p) d -> p i d", p=P))
-        nc.sync.dma_start(out=sin_sb[:], in_=sin.rearrange("(i p) d -> p i d", p=P))
         load_words("q", 512, 512, 0, 2)
         load_scales("q", 512, 1536)
         load_words("q", 512, 512, 2, 2)
@@ -126,20 +126,6 @@ def tile_attention_pa_kernel(
         warm = const.tile([P, 1], F32)
         nc.scalar.copy(out=warm[:], in_=identity[:, 0:1])
         table = const.tile([P, SEQ // P, BANK_HEADS, 4, HALF], F32)
-        for i in range(SEQ // P):
-            nc.gpsimd.tensor_scalar(
-                out=table[:, i, :, 0:4:3, :],
-                in0=cos_sb[:, i].rearrange("p (e j) -> p e j", j=HALF).unsqueeze(1).to_broadcast([P, BANK_HEADS, 2, HALF]),
-                scalar1=1.0, scalar2=0.0, op0=MULT, op1=ADD,
-            )
-            nc.gpsimd.tensor_scalar(
-                out=table[:, i, :, 1, :], in0=sin_sb[:, i, HALF:HD].unsqueeze(1).to_broadcast([P, BANK_HEADS, HALF]),
-                scalar1=1.0, scalar2=0.0, op0=MULT, op1=ADD,
-            )
-            nc.gpsimd.tensor_scalar(
-                out=table[:, i, :, 2, :], in0=sin_sb[:, i, 0:HALF].unsqueeze(1).to_broadcast([P, BANK_HEADS, HALF]),
-                scalar1=-1.0, scalar2=0.0, op0=MULT, op1=ADD,
-            )
 
         grouped_tiles = []
         x_codes = []
@@ -195,6 +181,19 @@ def tile_attention_pa_kernel(
         quantise(2)
         quantise(3)
 
+        for i in range(SEQ // P):
+            cosines = cos_sb[:, i].rearrange("p (e j) -> p e j", j=HALF)
+            nc.gpsimd.tensor_scalar(
+                out=table[:, i, :, 0:4:3, :], in0=cosines.unsqueeze(1).to_broadcast([P, BANK_HEADS, 2, HALF]),
+                scalar1=1.0, scalar2=0.0, op0=MULT, op1=ADD,
+            )
+            nc.scalar.copy(
+                out=table[:, i, :, 1, :], in_=sin_sb[:, i, HALF:HD].unsqueeze(1).to_broadcast([P, BANK_HEADS, HALF])
+            )
+            nc.scalar.mul(
+                out=table[:, i, :, 2, :], in_=sin_sb[:, i, 0:HALF].unsqueeze(1).to_broadcast([P, BANK_HEADS, HALF]), mul=-1.0
+            )
+
         def one_pass(name, col, n, m, g, out_ap):
             plane_col = weights[name]["plane_col"] + col
             nc.tensor.matmul_mx(
@@ -249,10 +248,10 @@ def tile_attention_pa_kernel(
         for m in range(TOKEN_TILES):
             bank = psum.tile([P, BANK], F32, tag="bank")
             first_banks.append(bank)
-        stages = [((0, 1), (0, 1)), ((0, 1), (2,)), ((2, 3), (0, 1, 2)), ((0, 1, 2, 3), (3,))]
+        stages = [((0,), (0, 1)), ((1,), (0, 1)), ((0, 1), (2,)), ((2, 3), (0, 1, 2)), ((0, 1, 2, 3), (3,))]
         for stage_passes, stage_tiles in stages:
-            for g in stage_passes:
-                for m in stage_tiles:
+            for m in stage_tiles:
+                for g in stage_passes:
                     one_pass("q", 0, BANK, m, g, first_banks[m][:])
         for m0 in (0, 2):
             finish_tiles_pair(0, m0, first_banks[m0 : m0 + 2])

from contextlib import ExitStack

import concourse.mybir as mybir
from concourse.masks import make_identity

BF16 = mybir.dt.bfloat16
F32 = mybir.dt.float32
I32 = mybir.dt.int32
U32 = mybir.dt.uint32
U8 = mybir.dt.uint8
FP8X4 = mybir.dt.float8_e4m3fn_x4
MULT = mybir.AluOpType.mult
ADD = mybir.AluOpType.add

P = 128
TOKENS = 512
SEQ = 256
D = 2048
PACK = 4
PASSES = D // (P * PACK)
TOKEN_TILES = TOKENS // P
HD = 128
HALF = HD // 2
BANK = 512
BANK_HEADS = BANK // HD
PSUM_BANKS = 8

FLOPS = 2 * TOKENS * D * (2048 + 1024 + 1024)


def tile_attention_pa_kernel(
    tc, x, cos, sin, Wq_words, Wq_scales, Wk_words, Wk_scales, Wv_words, Wv_scales, out_0, out_1, out_2
):
    nc = tc.nc
    x_rows = x.rearrange("b s d -> (b s) d")

    weights = {
        "q": dict(words=Wq_words, scales=Wq_scales, out=out_0, cols=2048, plane_col=0),
        "k": dict(words=Wk_words, scales=Wk_scales, out=out_1, cols=1024, plane_col=2048),
        "v": dict(words=Wv_words, scales=Wv_scales, out=out_2, cols=1024, plane_col=3072),
    }
    all_cols = 4096

    with ExitStack() as ctx:
        ctx.enter_context(tc.manual_schedule())
        const = ctx.enter_context(tc.tile_pool(name="const", bufs=1))
        x_pool = ctx.enter_context(tc.tile_pool(name="x", bufs=TOKEN_TILES))
        w_pool = ctx.enter_context(tc.tile_pool(name="w", bufs=1))
        terms_pool = ctx.enter_context(tc.tile_pool(name="terms", bufs=4))
        out_pool = ctx.enter_context(tc.tile_pool(name="out", bufs=1))
        psum = ctx.enter_context(tc.psum_pool(name="psum", bufs=PSUM_BANKS))

        zeros = const.tile([P, BANK], BF16)
        nc.vector.memset(zeros[:], 0.0)

        w_planes = const.tile([P, all_cols], U8, align_bytes=256)
        nc.vector.memset(w_planes[:, 0:BANK].bitcast(I32), 0)
        nc.vector.memset(w_planes[:, BANK:all_cols].bitcast(I32), 0)

        identity = const.tile([P, P], F32)
        make_identity(nc, identity[:])

        def idle_matmuls(bank_ap, n):
            for i in range(n):
                nc.tensor.matmul(out=bank_ap, lhsT=zeros[:, 0:P], rhs=zeros[:], start=True, stop=True)

        def load_scales(name, first, width):
            w = weights[name]
            cols = slice(w["plane_col"] + first, w["plane_col"] + first + width)
            rows = w["scales"].bitcast(I32)
            for quadrant in range(4):
                nc.sync.dma_start(
                    out=w_planes[32 * quadrant : 32 * quadrant + 16, cols].bitcast(I32),
                    in_=rows[:, 4 * quadrant : 4 * quadrant + 4, first // 4 : (first + width) // 4],
                )

        pieces = []

        def load_words(name, first, width, first_pass=0, n_passes=PASSES):
            words = w_pool.tile(
                [P, n_passes, width], U32, name="w_%s%d_%d" % (name, first, first_pass), align_bytes=256
            )
            view = weights[name]["words"].rearrange("g p n t -> p g (n t)").bitcast(I32)
            nc.sync.dma_start(
                out=words[:].bitcast(I32), in_=view[:, first_pass : first_pass + n_passes, first : first + width]
            )
            pieces.append((name, first, width, first_pass, n_passes, words))

        def moving(name, col, n, g):
            for piece_name, first, width, first_pass, n_passes, words in pieces:
                if piece_name == name and first <= col and col + n <= first + width:
                    if first_pass <= g and g < first_pass + n_passes:
                        return words[:, g - first_pass, col - first : col - first + n]
            return None

        x_tiles = []

        def load_x(m):
            x_sb = x_pool.tile([P, D], BF16)
            nc.sync.dma_start(out=x_sb[:], in_=x_rows[m * P : (m + 1) * P, :])
            x_tiles.append(x_sb)

        cos_sb = const.tile([P, SEQ // P, HD], BF16)
        sin_sb = const.tile([P, SEQ // P, HD], BF16)
        load_x(0)
        load_x(1)
        load_x(2)
        load_x(3)
        load_scales("q", 0, 512)
        load_words("q", 0, BANK, 0, 1)
        load_words("q", 0, BANK, 1, 1)
        nc.sync.dma_start(out=sin_sb[:], in_=sin.rearrange("(i p) d -> p i d", p=P))
        nc.sync.dma_start(out=cos_sb[:], in_=cos.rearrange("(i p) d -> p i d", p=P))
        load_words("q", 0, BANK, 2, 1)
        load_words("q", 0, BANK, 3, 1)
        load_words("q", 512, 512, 0, 2)
        load_scales("q", 512, 1536)
        load_words("q", 512, 512, 2, 2)
        load_words("q", 1024, 512)
        load_scales("k", 0, 1024)
        load_words("q", 1536, 512)
        load_scales("v", 0, 1024)
        load_words("k", 0, 1024)
        load_words("v", 0, 1024)

        warm = const.tile([P, 1], F32)
        nc.scalar.copy(out=warm[:], in_=identity[:, 0:1])
        table = const.tile([P, SEQ // P, BANK_HEADS, 4, HALF], F32)

        grouped_tiles = []
        x_codes = []
        x_scales = []

        sorted_tiles = []

        def sort_words(m):
            words = x_tiles[m][:].bitcast(F32)
            sorted_words = x_pool.tile([P, PASSES, 2, P], F32, bufs=2)
            nc.vector.tensor_copy(out=sorted_words[:], in_=words.rearrange("t (g p u) -> t g u p", g=PASSES, u=2))
            sorted_tiles.append(sorted_words)

        def turn(m, idle, is_sorted):
            words = x_tiles[m][:].bitcast(F32)
            grouped = x_pool.tile([P, PASSES, P, PACK], BF16, align_bytes=256)
            grouped_words = grouped[:].bitcast(F32)
            for pair in range(PASSES // 2):
                turned = psum.tile([P, 2, 2, P], F32, tag="bank")
                if pair == 0:
                    idle_matmuls(turned[:].rearrange("p g u t -> p (g u t)"), idle)
                for i in range(2):
                    first = (2 * pair + i) * 2 * P
                    for u in range(2):
                        if is_sorted:
                            block = sorted_tiles[m][:, 2 * pair + i, u, :]
                        else:
                            block = words[:, first + u : first + 2 * P : 2]
                        nc.tensor.transpose(turned[:, i, u, :], block, identity[:])
                nc.scalar.copy(out=grouped_words[:, 2 * pair : 2 * pair + 2], in_=turned[:].rearrange("p g u t -> p g t u"))
            grouped_tiles.append(grouped)

        def quantise(m):
            codes = x_pool.tile([P, PASSES, P], U32, align_bytes=256)
            scales = x_pool.tile([P, PASSES, P], U8, align_bytes=256)
            nc.vector.quantize_mx(
                out=codes[:].rearrange("p g t -> p (g t)").bitcast(FP8X4),
                scales=scales[:].rearrange("p g t -> p (g t)"),
                in_=grouped_tiles[m][:].rearrange("p g t c -> p (g t c)"),
            )
            x_codes.append(codes)
            x_scales.append(scales)

        sort_words(0)
        turn(0, 8, True)
        sort_words(1)
        turn(1, 2, True)
        sort_words(2)
        quantise(0)
        turn(2, 2, True)
        quantise(1)
        turn(3, 0, False)
        quantise(2)
        quantise(3)

        for i in range(SEQ // P):
            cosines = cos_sb[:, i].rearrange("p (e j) -> p e j", j=HALF)
            nc.gpsimd.tensor_scalar(
                out=table[:, i, :, 0:4:3, :], in0=cosines.unsqueeze(1).to_broadcast([P, BANK_HEADS, 2, HALF]),
                scalar1=1.0, scalar2=0.0, op0=MULT, op1=ADD,
            )
            nc.scalar.copy(
                out=table[:, i, :, 1, :], in_=sin_sb[:, i, HALF:HD].unsqueeze(1).to_broadcast([P, BANK_HEADS, HALF])
            )
            nc.scalar.mul(
                out=table[:, i, :, 2, :], in_=sin_sb[:, i, 0:HALF].unsqueeze(1).to_broadcast([P, BANK_HEADS, HALF]), mul=-1.0
            )

        def one_pass(name, col, n, m, g, out_ap):
            plane_col = weights[name]["plane_col"] + col
            nc.tensor.matmul_mx(
                out=out_ap,
                lhsT=x_codes[m][:, g, :].bitcast(FP8X4),
                lhsT_scale=x_scales[m][:, g, :],
                rhs=moving(name, col, n, g).bitcast(FP8X4),
                rhs_scale=w_planes[4 * g : P, plane_col : plane_col + n],
                start=(g == 0),
                stop=(g == PASSES - 1),
            )

        def project(name, col, n, m, out_ap):
            for g in range(PASSES):
                one_pass(name, col, n, m, g, out_ap)

        def products(bank, m, terms_ap):
            shape = [P, 2 * BANK_HEADS, 2, HALF]
            nc.vector.tensor_tensor(
                out=terms_ap.rearrange("p (c o j) -> p c o j", o=2, j=HALF),
                in0=bank[:].rearrange("p (c j) -> p c j", j=HALF).unsqueeze(2).to_broadcast(shape),
                in1=table[:, m % 2].rearrange("p h (s o) j -> p (h s) o j", o=2),
                op=MULT,
            )

        def add_terms(terms, result, engine):
            both = terms[:].rearrange("p b (h s d) -> p (b h) s d", s=2, d=HD)
            engine.tensor_tensor(
                out=result[:].rearrange("p b (h d) -> p (b h) d", d=HD), in0=both[:, :, 0, :], in1=both[:, :, 1, :], op=ADD
            )

        def out_rows(name):
            return weights[name]["out"].rearrange("b s h d -> (b s) (h d)")

        count = [0]

        def new_pair():
            count[0] += 1
            terms = terms_pool.tile([P, 2, 2 * BANK], F32, name="terms")
            result = out_pool.tile([P, 2, BANK], F32, name="result_%d" % count[0])
            return terms, result

        def finish_tiles_pair(col, m0, banks):
            terms, result = new_pair()
            for i in range(2):
                products(banks[i], m0 + i, terms[:, i, :])
            add_terms(terms, result, nc.gpsimd)
            rows = out_rows("q").rearrange("(m p) c -> p m c", p=P)
            nc.sync.dma_start(out=rows[:, m0 : m0 + 2, col : col + BANK], in_=result[:])

        first_banks = []
        for m in range(TOKEN_TILES):
            bank = psum.tile([P, BANK], F32, tag="bank")
            first_banks.append(bank)
        stages = [((0,), (0, 1)), ((1,), (0, 1)), ((0, 1), (2,)), ((2, 3), (0, 1, 2)), ((0, 1, 2, 3), (3,))]
        for stage_passes, stage_tiles in stages:
            for m in stage_tiles:
                for g in stage_passes:
                    one_pass("q", 0, BANK, m, g, first_banks[m][:])
        for m0 in (0, 2):
            finish_tiles_pair(0, m0, first_banks[m0 : m0 + 2])
        for col in (BANK, 2 * BANK, 3 * BANK):
            for m0 in (0, 2):
                pair_banks = []
                for i in range(2):
                    bank = psum.tile([P, BANK], F32, tag="bank")
                    project("q", col, BANK, m0 + i, bank[:])
                    pair_banks.append(bank)
                finish_tiles_pair(col, m0, pair_banks)

        def rope_unit(name, col, m, add_engine):
            terms, result = new_pair()
            for i in range(2):
                bank = psum.tile([P, BANK], F32, tag="bank")
                project(name, col + i * BANK, BANK, m, bank[:])
                products(bank, m, terms[:, i, :])
            add_terms(terms, result, add_engine)
            nc.sync.dma_start(
                out=out_rows(name)[m * P : (m + 1) * P, col : col + 2 * BANK], in_=result[:].rearrange("p b c -> p (b c)")
            )

        def copy_out(engine, out_ap, bank_ap):
            if engine == "scalar":
                nc.scalar.copy(out=out_ap, in_=bank_ap)
            else:
                nc.vector.tensor_copy(out=out_ap, in_=bank_ap)

        def plain_unit(name, col, m):
            copied = out_pool.tile([P, 2, BANK], F32, name="copied_%d" % m)
            for i in range(2):
                bank = psum.tile([P, BANK], F32, tag="bank")
                project(name, col + i * BANK, BANK, m, bank[:])
                copy_out("scalar", copied[:, i, :], bank[:])
            nc.scalar.dma_start(
                out=out_rows(name)[m * P : (m + 1) * P, col : col + 2 * BANK], in_=copied[:].rearrange("p b c -> p (b c)")
            )

        def last_unit(name, m, widths):
            first = 0
            for i, (width, engine) in enumerate(widths):
                copied = out_pool.tile([P, width], F32, name="last_%d" % i)
                bank = psum.tile([P, BANK], F32, tag="bank")
                project(name, first, width, m, bank[:, 0:width])
                copy_out(engine, copied[:], bank[:, 0:width])
                nc.sync.dma_start(out=out_rows(name)[m * P : (m + 1) * P, first : first + width], in_=copied[:])
                first += width

        rope_unit("k", 0, 0, nc.gpsimd)
        rope_unit("k", 0, 1, nc.gpsimd)
        plain_unit("v", 0, 0)
        rope_unit("k", 0, 2, nc.gpsimd)
        rope_unit("k", 0, 3, nc.vector)
        plain_unit("v", 0, 1)
        plain_unit("v", 0, 2)
        last_unit("v", 3, [(512, "scalar"), (256, "vector"), (128, "scalar"), (128, "vector")])
